import numpy as np
import ml_dtypes


def mxq(x, axis, fmt="e4m3"):
    dtype, down = {"e4m3": (ml_dtypes.float8_e4m3fn, 7), "e5m2": (ml_dtypes.float8_e5m2, 14)}[fmt]
    v = np.moveaxis(np.asarray(x, np.float32).astype(ml_dtypes.bfloat16).astype(np.float64), axis, -1)
    blocks = v.reshape(v.shape[:-1] + (-1, 32))
    amax = np.abs(blocks).max(-1, keepdims=True)
    byte = np.maximum(np.where(amax > 0, np.frexp(amax)[1] - 1 + 127, 0) - down, 1)
    scale = np.exp2(byte - 127.0)
    codes = (blocks / scale).astype(np.float32).astype(dtype).astype(np.float64)
    return np.moveaxis((codes * scale).reshape(v.shape), -1, axis)


WIDE = False


def mx_kscale(k):
    if not WIDE:
        return np.ones(k)
    levels = np.array([10, -10, 5, -5, 0])
    if k % 512:
        return np.exp2(np.random.permutation(np.resize(levels, k // 32))).repeat(32)
    a = np.empty((k // 512, 16))
    for p in range(k // 512):
        a[p, :8] = np.random.permutation(np.resize(levels, 8))
        for g in range(8):
            far = levels[np.abs(levels - a[p, g]) >= 10]
            a[p, g + 8] = far[np.random.randint(len(far))]
    return np.exp2(a.ravel()).repeat(32)


BF16 = ml_dtypes.bfloat16


def bf(x):
    return np.asarray(x, np.float32).astype(BF16)


def f64(x):
    return np.asarray(x).astype(np.float64)


N, C, H, W = 4, 1024, 32, 32

REPARAM_OFFSET = 2.0 ** -18
PEDESTAL = REPARAM_OFFSET ** 2
BETA_MIN = 1e-6
BOUND_BETA = (BETA_MIN + PEDESTAL) ** 0.5
BOUND_GAMMA = PEDESTAL ** 0.5
INVERSE = False


def nn_reparam(v, bound):
    return np.square(np.maximum(v, bound)) - PEDESTAL


def setup_inputs():
    u = np.exp2(np.round(np.log2(mx_kscale(C)) / 2))
    amp = np.exp(0.5 * np.random.standard_normal((N, 1, H, W)))
    x = np.random.standard_normal((N, C, H, W)) * amp * u[None, :, None, None]
    beta = np.random.standard_normal(C) * u
    gamma = np.random.standard_normal((C, C)) * 1.5 / np.sqrt(C) * u[:, None] / u[None, :]
    return {"x": bf(x), "beta": bf(beta), "gamma": bf(gamma)}


def reference(x, beta, gamma):
    x = f64(x)
    beta_eff = nn_reparam(f64(beta), BOUND_BETA)
    gamma_eff = nn_reparam(f64(gamma), BOUND_GAMMA)
    x2 = x * x
    denom_sq = (mxq(gamma_eff, 1, "e4m3") @ mxq(x2, 1, "e4m3").reshape(N, C, H * W)).reshape(N, C, H, W)
    denom_sq = denom_sq + beta_eff[None, :, None, None]
    norm = np.sqrt(denom_sq) if INVERSE else 1.0 / np.sqrt(denom_sq)
    return x * norm

@@ -1,0 +1,334 @@
+from contextlib import ExitStack
+
+import concourse.mybir as mybir
+from concourse.masks import make_identity
+
+F32 = mybir.dt.float32
+BF16 = mybir.dt.bfloat16
+U32 = mybir.dt.uint32
+U8 = mybir.dt.uint8
+FP8X4 = mybir.dt.float8_e4m3fn_x4
+ALU = mybir.AluOpType
+ACT = mybir.ActivationFunctionType
+
+P = 128
+NIMG = 4
+C = 1024
+HW = 1024
+FLOPS = 2 * NIMG * C * C * HW
+
+PEDESTAL = 2.0 ** -36
+BOUND_BETA = (1e-6 + PEDESTAL) ** 0.5
+
+WS = 304
+WS_LAST = 360
+LEAD = 7
+HALVES_FROM = 9
+NSLOT = 16
+
+
+def tile_einsumgdn_t_kernel(tc, x, beta, gamma, out):
+    nc = tc.nc
+    x_v = x.rearrange("n (g p j) h w -> n g p (j h w)", g=2, p=P, j=4)
+    x_c = x.rearrange("n (g p j) h w -> n g p j (h w)", g=2, p=P, j=4)
+    out_v = out.rearrange("n (g p s e) h w -> n g s p (e h w)", g=2, p=P, s=2, e=2)
+    gamma_v = gamma.rearrange("(g p s e) c -> g s p e c", g=2, p=P, s=2, e=2)
+    beta_v = beta.rearrange("(g p j) -> p g j", g=2, p=P, j=4)
+
+    pieces = [(0, 0, 0, 256, 256), (0, 0, 256, 256, 0), (0, 0, 512, 512, WS)]
+    for j in range(2, 16):
+        pieces.append((j // 4, (j // 2) % 2, 512 * (j % 2), 512, WS if j < 14 else WS_LAST))
+    npiece = len(pieces)
+    first_parts = [(0, 256), (256, 256), (512, 512)]
+
+    with ExitStack() as ctx:
+        const = ctx.enter_context(tc.tile_pool(name="const", bufs=1))
+        xpool = ctx.enter_context(tc.tile_pool(name="xpool", bufs=1))
+        gpool = ctx.enter_context(tc.tile_pool(name="gpool", bufs=2))
+        work = ctx.enter_context(tc.tile_pool(name="work", bufs=3))
+        opool = ctx.enter_context(tc.tile_pool(name="opool", bufs=5))
+        psum = ctx.enter_context(tc.psum_pool(name="psum", bufs=8))
+        ctx.enter_context(tc.manual_schedule())
+
+        graw = {}
+        for g in range(2):
+            graw[(0, g)] = gpool.tile([P, 2, 512], BF16, name="graw0%d" % g, bufs=1)
+        for t in range(1, 4):
+            graw[t] = gpool.tile([P, 2, C], BF16, name="graw", bufs=3)
+        xs = {}
+        xfirst = []
+        for q in range(3):
+            xfirst.append(xpool.tile([P, 4, first_parts[q][1]], BF16, name="xfirst%d" % q))
+        for n in range(NIMG):
+            for g in range(2):
+                if (n, g) != (0, 0):
+                    xs[(n, g)] = xpool.tile([P, 4, HW], BF16, name="xs%d%d" % (n, g))
+        bt = const.tile([P, 2, 4], BF16, name="bt")
+
+        def load_first(q):
+            w0, wd = first_parts[q]
+            nc.sync.dma_start(out=xfirst[q][:], in_=x_c[0, 0][:, :, w0 : w0 + wd])
+
+        nc.sync.dma_start(out=graw[(0, 0)][:], in_=gamma_v[0, 0][:, :, 0:512])
+        load_first(0)
+        nc.sync.dma_start(out=graw[(0, 1)][:], in_=gamma_v[0, 0][:, :, 512:1024])
+        load_first(1)
+        load_first(2)
+        for t in range(1, 4):
+            nc.sync.dma_start(out=graw[t][:], in_=gamma_v[t // 2, t % 2])
+        for n in range(NIMG):
+            for g in range(2):
+                if (n, g) != (0, 0):
+                    nc.sync.dma_start(
+                        out=xs[(n, g)][:].rearrange("p j w -> p (j w)"), in_=x_v[n, g]
+                    )
+            if n == 0:
+                with nc.allow_non_contiguous_dma(reason="beta: four channels a partition, twice"):
+                    nc.sync.dma_start(out=bt[:], in_=beta_v)
+
+        warm = const.tile([P, 1], F32, name="warm")
+        warm2 = const.tile([P, 1], F32, name="warm2")
+        nc.vector.memset(warm[:], 1.0)
+        nc.scalar.activation(out=warm2[:], in_=warm[:], func=ACT.Abs_reciprocal_sqrt)
+
+        ident = const.tile([P, P], F32, name="ident")
+        make_identity(nc, ident[:])
+
+        gcodes = const.tile([P, 4, 512], U32, name="gcodes", align_bytes=64)
+        gsc = const.tile([P, 4, 512], U8, name="gsc", align_bytes=64)
+        grelu = {}
+        gbank = {}
+        gsq = {}
+        gg = {}
+
+        def g_relu(key):
+            if key in (1, 2, 3):
+                grelu[key] = gpool.tile([P, 2, C], BF16, name="grelu", bufs=3)
+            else:
+                grelu[key] = gpool.tile([P, 2, 512], BF16, name="grelu0%d" % key[1], bufs=1)
+            nc.vector.tensor_scalar(
+                out=grelu[key][:], in0=graw[key][:], scalar1=0.0, scalar2=None, op0=ALU.max
+            )
+
+        def g_transpose(t, g):
+            src = grelu[(0, g)] if t == 0 else grelu[t]
+            gw = src[:].rearrange("p e c -> p (e c)").bitcast(F32)
+            bank = psum.tile([P, 512], F32, name="bank")
+            for u in range(2):
+                for e1 in range(2):
+                    src0 = (256 * e1) if t == 0 else (512 * e1 + 256 * g)
+                    dst0 = 256 * u + 128 * e1
+                    nc.tensor.transpose(
+                        bank[:, dst0 : dst0 + 128], gw[:, src0 + u : src0 + 256 : 2], ident[:]
+                    )
+            gbank[(t, g)] = bank
+
+        def g_square(t, g):
+            sq = work.tile([P, 1024], F32, name="sq", bufs=4)
+            nc.scalar.activation(
+                out=sq[:].rearrange("p (j u e) -> p j u e", u=2, e=2),
+                in_=gbank[(t, g)][:].bitcast(BF16).rearrange("p (u j e) -> p j u e", u=2, e=2),
+                func=ACT.Square,
+            )
+            gsq[(t, g)] = sq
+
+        def g_sub(t, g):
+            if g == 0:
+                gg[t] = gpool.tile([P, 2, 1024], BF16, name="gg", bufs=3, align_bytes=64)
+            nc.vector.tensor_scalar(
+                out=gg[t][:, g, :], in0=gsq[(t, g)][:], scalar1=-PEDESTAL, scalar2=0.0,
+                op0=ALU.add, op1=ALU.max,
+            )
+
+        def g_quant(t):
+            nc.vector.quantize_mx(
+                out=gcodes[:, t, :].bitcast(FP8X4),
+                scales=gsc[:, t, :],
+                in_=gg[t][:].rearrange("p g k -> p (g k)"),
+            )
+
+        xcodes = {}
+        xsc = {}
+        grp = {}
+
+        def sq_tile(j):
+            if j not in grp:
+                grp[j] = work.tile([P, 512, 4], BF16, name="grp", bufs=4, align_bytes=64)
+            return grp[j]
+
+        def sq_source(j, c0, c1):
+            n, g, w0, wd, ws = pieces[j]
+            if j < 3:
+                return xfirst[j][:, :, c0:c1]
+            return xs[(n, g)][:, :, w0 + c0 : w0 + c1]
+
+        def sq_scalar(j):
+            n, g, w0, wd, ws = pieces[j]
+            if ws > 0:
+                nc.scalar.activation(
+                    out=sq_tile(j)[:, 0:ws, :].rearrange("p (c i) t -> p c t i", i=4),
+                    in_=sq_source(j, 0, ws).rearrange("p t (c i) -> p c t i", i=4),
+                    func=ACT.Square,
+                )
+
+        def sq_vector(j):
+            n, g, w0, wd, ws = pieces[j]
+            if ws < wd:
+                vsrc = sq_source(j, ws, wd).rearrange("p t (c i) -> p c t i", i=4)
+                nc.vector.tensor_tensor(
+                    out=sq_tile(j)[:, ws:wd, :].rearrange("p (c i) t -> p c t i", i=4),
+                    in0=vsrc, in1=vsrc, op=ALU.mult,
+                )
+
+        def sq_quant(j):
+            n, g, w0, wd, ws = pieces[j]
+            if n not in xcodes:
+                xcodes[n] = work.tile([P, 2, HW], U32, name="xcodes", align_bytes=64)
+                xsc[n] = work.tile([P, 2, HW], U8, name="xsc", align_bytes=64)
+            nc.vector.quantize_mx(
+                out=xcodes[n][:, g, w0 : w0 + wd].bitcast(FP8X4),
+                scales=xsc[n][:, g, w0 : w0 + wd],
+                in_=grp[j][:, 0:wd, :].rearrange("p w t -> p (w t)"),
+            )
+
+        acc = {}
+        otile = {}
+
+        def mm(k):
+            n, t = k // 4, k % 4
+            for e1 in range(2):
+                for h in range(2):
+                    bank = psum.tile([P, 512], F32, name="bank")
+                    acc[(k, e1, h)] = bank
+                    for g in range(2):
+                        m0 = 256 * g + 128 * e1
+                        nc.tensor.matmul_mx(
+                            out=bank[:],
+                            lhsT=gcodes[:, t, m0 : m0 + 128].bitcast(FP8X4),
+                            lhsT_scale=gsc[:, t, m0 : m0 + 128],
+                            rhs=xcodes[n][:, g, 512 * h : 512 * h + 512].bitcast(FP8X4),
+                            rhs_scale=xsc[n][:, g, 512 * h : 512 * h + 512],
+                            start=(g == 0),
+                            stop=(g == 1),
+                        )
+
+        def rsq(k):
+            t = k % 4
+            otile[k] = opool.tile([P, 2 * HW], F32, name="o")
+            for e1 in range(2):
+                for h in range(2):
+                    c0 = HW * e1 + 512 * h
+                    nc.scalar.activation(
+                        out=otile[k][:, c0 : c0 + 512],
+                        in_=acc[(k, e1, h)][:],
+                        func=ACT.Abs_reciprocal_sqrt,
+                        bias=beff[:, 2 * t + e1 : 2 * t + e1 + 1],
+                        scale=1.0,
+                    )
+
+        def finish(k, b0, b1):
+            n, t = k // 4, k % 4
+            r0 = 2 * (t % 2)
+            cols = slice(512 * b0, 512 * b1)
+            if (n, t // 2) == (0, 0):
+                o3 = otile[k][:].rearrange("p (e w) -> p e w", e=2)
+                for q in range(3):
+                    w0, wd = first_parts[q]
+                    nc.vector.tensor_tensor(
+                        out=o3[:, :, w0 : w0 + wd], in0=o3[:, :, w0 : w0 + wd],
+                        in1=xfirst[q][:, r0 : r0 + 2, :], op=ALU.mult,
+                    )
+            else:
+                xrow = xs[(n, t // 2)][:, r0 : r0 + 2, :].rearrange("p e w -> p (e w)")
+                nc.vector.tensor_tensor(
+                    out=otile[k][:, cols], in0=otile[k][:, cols], in1=xrow[:, cols], op=ALU.mult
+                )
+            nc.sync.dma_start(out=out_v[n, t // 2, t % 2][:, cols], in_=otile[k][:, cols])
+
+        g_relu((0, 0))
+        g_transpose(0, 0)
+        sq_scalar(0)
+        g_relu((0, 1))
+        g_transpose(0, 1)
+        g_square(0, 0)
+        g_square(0, 1)
+        sq_quant(0)
+        sq_vector(1)
+        sq_vector(2)
+        sq_scalar(2)
+        g_relu(1)
+        g_transpose(1, 0)
+        g_transpose(1, 1)
+        g_sub(0, 0)
+        g_relu(2)
+        g_transpose(2, 0)
+        g_transpose(2, 1)
+        g_sub(0, 1)
+        g_square(1, 0)
+        g_square(1, 1)
+        g_relu(3)
+        g_transpose(3, 0)
+        g_transpose(3, 1)
+        sq_quant(1)
+        g_quant(0)
+        sq_quant(2)
+        g_sub(1, 0)
+        g_sub(1, 1)
+        g_square(2, 0)
+        g_square(2, 1)
+        sq_vector(3)
+        g_quant(1)
+        g_sub(2, 0)
+        g_sub(2, 1)
+        g_square(3, 0)
+        g_square(3, 1)
+        sq_vector(4)
+        g_quant(2)
+        sq_scalar(3)
+        sq_scalar(4)
+        g_sub(3, 0)
+        g_sub(3, 1)
+        sq_quant(3)
+
+        bmax = const.tile([P, 8], F32, name="bmax")
+        beff = const.tile([P, 8], F32, name="beff")
+        nc.vector.tensor_scalar(
+            out=bmax[:], in0=bt[:].rearrange("p g j -> p (g j)"),
+            scalar1=BOUND_BETA, scalar2=None, op0=ALU.max,
+        )
+        nc.vector.tensor_tensor(out=beff[:], in0=bmax[:], in1=bmax[:], op=ALU.mult)
+        nc.vector.tensor_scalar(
+            out=beff[:], in0=beff[:], scalar1=-PEDESTAL, scalar2=None, op0=ALU.add
+        )
+        g_quant(3)
+        sq_quant(4)
+
+        vnext = 5
+        qnext = 5
+        for j in range(5, LEAD):
+            sq_scalar(j)
+            while vnext <= j + 1:
+                sq_vector(vnext)
+                vnext += 1
+            if qnext < j:
+                sq_quant(qnext)
+                qnext += 1
+
+        for k in range(NSLOT):
+            j = k + LEAD
+            if j < npiece:
+                sq_scalar(j)
+            mm(k)
+            rsq(k)
+            if k >= 1:
+                finish(k - 1, 2 if k - 1 >= HALVES_FROM else 0, 4)
+            while vnext <= j + 1 and vnext < npiece:
+                sq_vector(vnext)
+                vnext += 1
+            if qnext < npiece:
+                sq_quant(qnext)
+                qnext += 1
+            if HALVES_FROM <= k < NSLOT - 1:
+                finish(k, 0, 2)
+        for b in range(4):
+            finish(NSLOT - 1, b, b + 1)

@@ -22,9 +22,14 @@ BOUND_BETA = (1e-6 + PEDESTAL) ** 0.5
 
 WS = 304
 WS_LAST = 360
+WG = 192
+WS_G = 224
+GFIRST = 9
+GRP_BUFS = 3
 LEAD = 7
 HALVES_FROM = 9
 NSLOT = 16
+NXB = 12
 
 
 def tile_einsumgdn_t_kernel(tc, x, beta, gamma, out):
@@ -37,8 +42,9 @@ def tile_einsumgdn_t_kernel(tc, x, beta, gamma, out):
 
     pieces = [(0, 0, 0, 256, 256), (0, 0, 256, 256, 0), (0, 0, 512, 512, WS)]
     for j in range(2, 16):
-        pieces.append((j // 4, (j // 2) % 2, 512 * (j % 2), 512, WS if j < 14 else WS_LAST))
+        pieces.append((j // 4, (j // 2) % 2, 512 * (j % 2), 512, WS if j + 1 < GFIRST else WS_G))
     npiece = len(pieces)
+    gshare = [WG if j >= GFIRST else 0 for j in range(npiece)]
     first_parts = [(0, 256), (256, 256), (512, 512)]
 
     with ExitStack() as ctx:
@@ -93,6 +99,8 @@ def tile_einsumgdn_t_kernel(tc, x, beta, gamma, out):
 
         ident = const.tile([P, P], F32, name="ident")
         make_identity(nc, ident[:])
+        identb = const.tile([P, P], BF16, name="identb")
+        make_identity(nc, identb[:])
 
         gcodes = const.tile([P, 4, 512], U32, name="gcodes", align_bytes=64)
         gsc = const.tile([P, 4, 512], U8, name="gsc", align_bytes=64)
@@ -153,7 +161,7 @@ def tile_einsumgdn_t_kernel(tc, x, beta, gamma, out):
 
         def sq_tile(j):
             if j not in grp:
-                grp[j] = work.tile([P, 512, 4], BF16, name="grp", bufs=4, align_bytes=64)
+                grp[j] = work.tile([P, 512, 4], BF16, name="grp", bufs=GRP_BUFS, align_bytes=64)
             return grp[j]
 
         def sq_source(j, c0, c1):
@@ -173,12 +181,20 @@ def tile_einsumgdn_t_kernel(tc, x, beta, gamma, out):
 
         def sq_vector(j):
             n, g, w0, wd, ws = pieces[j]
-            if ws < wd:
-                vsrc = sq_source(j, ws, wd).rearrange("p t (c i) -> p c t i", i=4)
+            we = wd - gshare[j]
+            if ws < we:
+                vsrc = sq_source(j, ws, we).rearrange("p t (c i) -> p c t i", i=4)
                 nc.vector.tensor_tensor(
-                    out=sq_tile(j)[:, ws:wd, :].rearrange("p (c i) t -> p c t i", i=4),
+                    out=sq_tile(j)[:, ws:we, :].rearrange("p (c i) t -> p c t i", i=4),
                     in0=vsrc, in1=vsrc, op=ALU.mult,
                 )
+
+        def sq_gpsimd(j):
+            n, g, w0, wd, ws = pieces[j]
+            gsrc = sq_source(j, wd - gshare[j], wd).rearrange("p t w -> p w t")
+            nc.gpsimd.tensor_tensor(
+                out=sq_tile(j)[:, wd - gshare[j] : wd, :], in0=gsrc, in1=gsrc, op=ALU.mult
+            )
 
         def sq_quant(j):
             n, g, w0, wd, ws = pieces[j]
@@ -212,6 +228,29 @@ def tile_einsumgdn_t_kernel(tc, x, beta, gamma, out):
                             stop=(g == 1),
                         )
 
+        xb = {}
+
+        def xcopy(k):
+            n, t = k // 4, k % 4
+            r0 = 2 * (t % 2)
+            for e1 in range(2):
+                bank = psum.tile([P, HW], BF16, name="bank")
+                xb[(k, e1)] = bank
+                if (n, t // 2) == (0, 0):
+                    for q in range(3):
+                        w0, wd = first_parts[q]
+                        nc.tensor.matmul(
+                            out=bank[:, w0 : w0 + wd], lhsT=identb[:], rhs=xfirst[q][:, r0 + e1, :],
+                            start=True, stop=True,
+                        )
+                else:
+                    for h in range(2):
+                        nc.tensor.matmul(
+                            out=bank[:, 512 * h : 512 * h + 512], lhsT=identb[:],
+                            rhs=xs[(n, t // 2)][:, r0 + e1, 512 * h : 512 * h + 512],
+                            start=True, stop=True,
+                        )
+
         def rsq(k):
             t = k % 4
             otile[k] = opool.tile([P, 2 * HW], F32, name="o")
@@ -230,13 +269,11 @@ def tile_einsumgdn_t_kernel(tc, x, beta, gamma, out):
             n, t = k // 4, k % 4
             r0 = 2 * (t % 2)
             cols = slice(512 * b0, 512 * b1)
-            if (n, t // 2) == (0, 0):
-                o3 = otile[k][:].rearrange("p (e w) -> p e w", e=2)
-                for q in range(3):
-                    w0, wd = first_parts[q]
+            if k < NXB:
+                for e1 in range(b0 // 2, b1 // 2):
+                    row = slice(HW * e1, HW * e1 + HW)
                     nc.vector.tensor_tensor(
-                        out=o3[:, :, w0 : w0 + wd], in0=o3[:, :, w0 : w0 + wd],
-                        in1=xfirst[q][:, r0 : r0 + 2, :], op=ALU.mult,
+                        out=otile[k][:, row], in0=otile[k][:, row], in1=xb[(k, e1)][:], op=ALU.mult
                     )
             else:
                 xrow = xs[(n, t // 2)][:, r0 : r0 + 2, :].rearrange("p e w -> p (e w)")
@@ -319,6 +356,8 @@ def tile_einsumgdn_t_kernel(tc, x, beta, gamma, out):
             if j < npiece:
                 sq_scalar(j)
             mm(k)
+            if k < NXB:
+                xcopy(k)
             rsq(k)
             if k >= 1:
                 finish(k - 1, 2 if k - 1 >= HALVES_FROM else 0, 4)
@@ -327,6 +366,8 @@ def tile_einsumgdn_t_kernel(tc, x, beta, gamma, out):
                 vnext += 1
             if qnext < npiece:
                 sq_quant(qnext)
+                if qnext + GRP_BUFS < npiece:
+                    sq_gpsimd(qnext + GRP_BUFS)
                 qnext += 1
             if HALVES_FROM <= k < NSLOT - 1:
                 finish(k, 0, 2)

@@ -20,16 +20,16 @@ FLOPS = 2 * NIMG * C * C * HW
 PEDESTAL = 2.0 ** -36
 BOUND_BETA = (1e-6 + PEDESTAL) ** 0.5
 
-WS = 304
-WS_LAST = 360
-WG = 192
-WS_G = 224
-GFIRST = 9
-GRP_BUFS = 3
-LEAD = 7
-HALVES_FROM = 9
 NSLOT = 16
-NXB = 12
+WS_HEAD = 428
+WS_EARLY = 220
+WS_G = 256
+WS_END = 256
+NEND = 0
+WG = 192
+GRP_BUFS = 3
+QLEAD = 5
+NXB = 9
 
 
 def tile_einsumgdn_t_kernel(tc, x, beta, gamma, out):
@@ -40,12 +40,29 @@ def tile_einsumgdn_t_kernel(tc, x, beta, gamma, out):
     gamma_v = gamma.rearrange("(g p s e) c -> g s p e c", g=2, p=P, s=2, e=2)
     beta_v = beta.rearrange("(g p j) -> p g j", g=2, p=P, j=4)
 
-    pieces = [(0, 0, 0, 256, 256), (0, 0, 256, 256, 0), (0, 0, 512, 512, WS)]
-    for j in range(2, 16):
-        pieces.append((j // 4, (j // 2) % 2, 512 * (j % 2), 512, WS if j + 1 < GFIRST else WS_G))
+    pieces = [(0, 0, 0, 256), (0, 0, 256, 256), (0, 0, 512, 512), (0, 1, 0, 512), (0, 1, 512, 512)]
+    for n in range(1, NIMG):
+        for g in range(2):
+            for h in range(2):
+                pieces.append((n, g, 512 * h, 512))
     npiece = len(pieces)
-    gshare = [WG if j >= GFIRST else 0 for j in range(npiece)]
-    first_parts = [(0, 256), (256, 256), (512, 512)]
+    gfirst = QLEAD + GRP_BUFS
+    sshare = []
+    gshare = []
+    for j in range(npiece):
+        gshare.append(WG if j >= gfirst else 0)
+        if j == 0:
+            sshare.append(256)
+        elif j == 1:
+            sshare.append(0)
+        elif j < 5:
+            sshare.append(WS_HEAD)
+        elif j < gfirst:
+            sshare.append(WS_EARLY)
+        elif j < npiece - NEND:
+            sshare.append(WS_G)
+        else:
+            sshare.append(WS_END)
 
     with ExitStack() as ctx:
         const = ctx.enter_context(tc.tile_pool(name="const", bufs=1))
@@ -53,7 +70,7 @@ def tile_einsumgdn_t_kernel(tc, x, beta, gamma, out):
         gpool = ctx.enter_context(tc.tile_pool(name="gpool", bufs=2))
         work = ctx.enter_context(tc.tile_pool(name="work", bufs=3))
         opool = ctx.enter_context(tc.tile_pool(name="opool", bufs=5))
-        psum = ctx.enter_context(tc.psum_pool(name="psum", bufs=8))
+        psum = ctx.enter_context(tc.psum_pool(name="psum", bufs=4))
         ctx.enter_context(tc.manual_schedule())
 
         graw = {}
@@ -61,36 +78,36 @@ def tile_einsumgdn_t_kernel(tc, x, beta, gamma, out):
             graw[(0, g)] = gpool.tile([P, 2, 512], BF16, name="graw0%d" % g, bufs=1)
         for t in range(1, 4):
             graw[t] = gpool.tile([P, 2, C], BF16, name="graw", bufs=3)
+        xpart = {}
+        for j in range(5):
+            xpart[j] = xpool.tile([P, 4, pieces[j][3]], BF16, name="xpart%d" % j)
         xs = {}
-        xfirst = []
-        for q in range(3):
-            xfirst.append(xpool.tile([P, 4, first_parts[q][1]], BF16, name="xfirst%d" % q))
-        for n in range(NIMG):
+        for n in range(1, NIMG):
             for g in range(2):
-                if (n, g) != (0, 0):
-                    xs[(n, g)] = xpool.tile([P, 4, HW], BF16, name="xs%d%d" % (n, g))
+                xs[(n, g)] = xpool.tile([P, 4, HW], BF16, name="xs%d%d" % (n, g))
         bt = const.tile([P, 2, 4], BF16, name="bt")
 
-        def load_first(q):
-            w0, wd = first_parts[q]
-            nc.sync.dma_start(out=xfirst[q][:], in_=x_c[0, 0][:, :, w0 : w0 + wd])
+        def load_part(j):
+            n, g, w0, wd = pieces[j]
+            nc.sync.dma_start(out=xpart[j][:], in_=x_c[0, g][:, :, w0 : w0 + wd])
 
         nc.sync.dma_start(out=graw[(0, 0)][:], in_=gamma_v[0, 0][:, :, 0:512])
-        load_first(0)
+        load_part(0)
         nc.sync.dma_start(out=graw[(0, 1)][:], in_=gamma_v[0, 0][:, :, 512:1024])
-        load_first(1)
-        load_first(2)
-        for t in range(1, 4):
-            nc.sync.dma_start(out=graw[t][:], in_=gamma_v[t // 2, t % 2])
-        for n in range(NIMG):
+        load_part(1)
+        load_part(2)
+        load_part(3)
+        load_part(4)
+        nc.sync.dma_start(out=graw[1][:], in_=gamma_v[0, 1])
+        with nc.allow_non_contiguous_dma(reason="beta: four channels a partition, twice"):
+            nc.sync.dma_start(out=bt[:], in_=beta_v)
+        nc.sync.dma_start(out=xs[(1, 0)][:].rearrange("p j w -> p (j w)"), in_=x_v[1, 0])
+        nc.sync.dma_start(out=graw[2][:], in_=gamma_v[1, 0])
+        nc.sync.dma_start(out=graw[3][:], in_=gamma_v[1, 1])
+        for n in range(1, NIMG):
             for g in range(2):
-                if (n, g) != (0, 0):
-                    nc.sync.dma_start(
-                        out=xs[(n, g)][:].rearrange("p j w -> p (j w)"), in_=x_v[n, g]
-                    )
-            if n == 0:
-                with nc.allow_non_contiguous_dma(reason="beta: four channels a partition, twice"):
-                    nc.sync.dma_start(out=bt[:], in_=beta_v)
+                if (n, g) != (1, 0):
+                    nc.sync.dma_start(out=xs[(n, g)][:].rearrange("p j w -> p (j w)"), in_=x_v[n, g])
 
         warm = const.tile([P, 1], F32, name="warm")
         warm2 = const.tile([P, 1], F32, name="warm2")
@@ -121,7 +138,7 @@ def tile_einsumgdn_t_kernel(tc, x, beta, gamma, out):
         def g_transpose(t, g):
             src = grelu[(0, g)] if t == 0 else grelu[t]
             gw = src[:].rearrange("p e c -> p (e c)").bitcast(F32)
-            bank = psum.tile([P, 512], F32, name="bank")
+            bank = psum.tile([P, 512], F32, name="aux")
             for u in range(2):
                 for e1 in range(2):
                     src0 = (256 * e1) if t == 0 else (512 * e1 + 256 * g)
@@ -165,13 +182,13 @@ def tile_einsumgdn_t_kernel(tc, x, beta, gamma, out):
             return grp[j]
 
         def sq_source(j, c0, c1):
-            n, g, w0, wd, ws = pieces[j]
-            if j < 3:
-                return xfirst[j][:, :, c0:c1]
+            n, g, w0, wd = pieces[j]
+            if n == 0:
+                return xpart[j][:, :, c0:c1]
             return xs[(n, g)][:, :, w0 + c0 : w0 + c1]
 
         def sq_scalar(j):
-            n, g, w0, wd, ws = pieces[j]
+            ws = sshare[j]
             if ws > 0:
                 nc.scalar.activation(
                     out=sq_tile(j)[:, 0:ws, :].rearrange("p (c i) t -> p c t i", i=4),
@@ -180,8 +197,8 @@ def tile_einsumgdn_t_kernel(tc, x, beta, gamma, out):
                 )
 
         def sq_vector(j):
-            n, g, w0, wd, ws = pieces[j]
-            we = wd - gshare[j]
+            ws = sshare[j]
+            we = pieces[j][3] - gshare[j]
             if ws < we:
                 vsrc = sq_source(j, ws, we).rearrange("p t (c i) -> p c t i", i=4)
                 nc.vector.tensor_tensor(
@@ -190,14 +207,14 @@ def tile_einsumgdn_t_kernel(tc, x, beta, gamma, out):
                 )
 
         def sq_gpsimd(j):
-            n, g, w0, wd, ws = pieces[j]
+            wd = pieces[j][3]
             gsrc = sq_source(j, wd - gshare[j], wd).rearrange("p t w -> p w t")
             nc.gpsimd.tensor_tensor(
                 out=sq_tile(j)[:, wd - gshare[j] : wd, :], in0=gsrc, in1=gsrc, op=ALU.mult
             )
 
         def sq_quant(j):
-            n, g, w0, wd, ws = pieces[j]
+            n, g, w0, wd = pieces[j]
             if n not in xcodes:
                 xcodes[n] = work.tile([P, 2, HW], U32, name="xcodes", align_bytes=64)
                 xsc[n] = work.tile([P, 2, HW], U8, name="xsc", align_bytes=64)
@@ -209,12 +226,13 @@ def tile_einsumgdn_t_kernel(tc, x, beta, gamma, out):
 
         acc = {}
         otile = {}
+        xb = {}
 
         def mm(k):
             n, t = k // 4, k % 4
             for e1 in range(2):
                 for h in range(2):
-                    bank = psum.tile([P, 512], F32, name="bank")
+                    bank = psum.tile([P, 512], F32, name="acc")
                     acc[(k, e1, h)] = bank
                     for g in range(2):
                         m0 = 256 * g + 128 * e1
@@ -228,21 +246,20 @@ def tile_einsumgdn_t_kernel(tc, x, beta, gamma, out):
                             stop=(g == 1),
                         )
 
-        xb = {}
-
         def xcopy(k):
             n, t = k // 4, k % 4
             r0 = 2 * (t % 2)
             for e1 in range(2):
-                bank = psum.tile([P, HW], BF16, name="bank")
+                bank = psum.tile([P, HW], BF16, name="aux")
                 xb[(k, e1)] = bank
-                if (n, t // 2) == (0, 0):
-                    for q in range(3):
-                        w0, wd = first_parts[q]
-                        nc.tensor.matmul(
-                            out=bank[:, w0 : w0 + wd], lhsT=identb[:], rhs=xfirst[q][:, r0 + e1, :],
-                            start=True, stop=True,
-                        )
+                if n == 0:
+                    for j in range(5):
+                        if pieces[j][1] == t // 2:
+                            w0, wd = pieces[j][2], pieces[j][3]
+                            nc.tensor.matmul(
+                                out=bank[:, w0 : w0 + wd], lhsT=identb[:], rhs=xpart[j][:, r0 + e1, :],
+                                start=True, stop=True,
+                            )
                 else:
                     for h in range(2):
                         nc.tensor.matmul(
@@ -289,44 +306,23 @@ def tile_einsumgdn_t_kernel(tc, x, beta, gamma, out):
         g_transpose(0, 1)
         g_square(0, 0)
         g_square(0, 1)
-        sq_quant(0)
         sq_vector(1)
+        sq_quant(0)
         sq_vector(2)
         sq_scalar(2)
+        g_sub(0, 0)
+        sq_quant(1)
+        g_sub(0, 1)
+        sq_vector(3)
+        sq_scalar(3)
+        sq_quant(2)
+        g_quant(0)
         g_relu(1)
         g_transpose(1, 0)
         g_transpose(1, 1)
-        g_sub(0, 0)
-        g_relu(2)
-        g_transpose(2, 0)
-        g_transpose(2, 1)
-        g_sub(0, 1)
-        g_square(1, 0)
-        g_square(1, 1)
-        g_relu(3)
-        g_transpose(3, 0)
-        g_transpose(3, 1)
-        sq_quant(1)
-        g_quant(0)
-        sq_quant(2)
-        g_sub(1, 0)
-        g_sub(1, 1)
-        g_square(2, 0)
-        g_square(2, 1)
-        sq_vector(3)
-        g_quant(1)
-        g_sub(2, 0)
-        g_sub(2, 1)
-        g_square(3, 0)
-        g_square(3, 1)
         sq_vector(4)
-        g_quant(2)
-        sq_scalar(3)
         sq_scalar(4)
-        g_sub(3, 0)
-        g_sub(3, 1)
         sq_quant(3)
-
         bmax = const.tile([P, 8], F32, name="bmax")
         beff = const.tile([P, 8], F32, name="beff")
         nc.vector.tensor_scalar(
@@ -337,39 +333,38 @@ def tile_einsumgdn_t_kernel(tc, x, beta, gamma, out):
         nc.vector.tensor_scalar(
             out=beff[:], in0=beff[:], scalar1=-PEDESTAL, scalar2=None, op0=ALU.add
         )
-        g_quant(3)
+        sq_vector(5)
+        g_relu(2)
         sq_quant(4)
 
-        vnext = 5
-        qnext = 5
-        for j in range(5, LEAD):
-            sq_scalar(j)
-            while vnext <= j + 1:
-                sq_vector(vnext)
-                vnext += 1
-            if qnext < j:
-                sq_quant(qnext)
-                qnext += 1
-
         for k in range(NSLOT):
-            j = k + LEAD
-            if j < npiece:
-                sq_scalar(j)
+            if k < 3:
+                g_square(k + 1, 0)
+                g_square(k + 1, 1)
+            if k + QLEAD < npiece:
+                sq_scalar(k + QLEAD)
             mm(k)
-            if k < NXB:
-                xcopy(k)
             rsq(k)
             if k >= 1:
-                finish(k - 1, 2 if k - 1 >= HALVES_FROM else 0, 4)
-            while vnext <= j + 1 and vnext < npiece:
-                sq_vector(vnext)
-                vnext += 1
-            if qnext < npiece:
-                sq_quant(qnext)
-                if qnext + GRP_BUFS < npiece:
-                    sq_gpsimd(qnext + GRP_BUFS)
-                qnext += 1
-            if HALVES_FROM <= k < NSLOT - 1:
-                finish(k, 0, 2)
+                finish(k - 1, 0, 2)
+                finish(k - 1, 2, 4)
+            if k < NXB:
+                xcopy(k)
+            if k < 2:
+                g_transpose(k + 2, 0)
+                g_transpose(k + 2, 1)
+            if k < 3:
+                g_sub(k + 1, 0)
+                g_sub(k + 1, 1)
+            if k + QLEAD + 1 < npiece:
+                sq_vector(k + QLEAD + 1)
+            if k < 3:
+                g_quant(k + 1)
+            if k == 0:
+                g_relu(3)
+            if k + QLEAD < npiece:
+                sq_quant(k + QLEAD)
+                if k + QLEAD + GRP_BUFS < npiece:
+                    sq_gpsimd(k + QLEAD + GRP_BUFS)
         for b in range(4):
             finish(NSLOT - 1, b, b + 1)

@@ -21,12 +21,12 @@ PEDESTAL = 2.0 ** -36
 BOUND_BETA = (1e-6 + PEDESTAL) ** 0.5
 
 NSLOT = 16
-WS_HEAD = 428
+WS_HEAD = 396
 WS_EARLY = 220
-WS_G = 256
-WS_END = 256
+WS_G = 240
+WS_END = 240
 NEND = 0
-WG = 192
+WG = 224
 GRP_BUFS = 3
 QLEAD = 5
 NXB = 9

@@ -21,12 +21,12 @@ PEDESTAL = 2.0 ** -36
 BOUND_BETA = (1e-6 + PEDESTAL) ** 0.5
 
 NSLOT = 16
-WS_HEAD = 396
-WS_EARLY = 220
-WS_G = 240
-WS_END = 240
+WS_HEAD = 364
+WS_EARLY = 280
+WS_G = 224
+WS_END = 224
 NEND = 0
-WG = 224
+WG = 208
 GRP_BUFS = 3
 QLEAD = 5
 NXB = 9

@@ -21,13 +21,14 @@ PEDESTAL = 2.0 ** -36
 BOUND_BETA = (1e-6 + PEDESTAL) ** 0.5
 
 NSLOT = 16
-WS_HEAD = 364
+WS_HEAD = 368
 WS_EARLY = 280
 WS_G = 224
 WS_END = 224
 NEND = 0
 WG = 208
 GRP_BUFS = 3
+RUN = 8
 QLEAD = 5
 NXB = 9
 
@@ -191,8 +192,8 @@ def tile_einsumgdn_t_kernel(tc, x, beta, gamma, out):
             ws = sshare[j]
             if ws > 0:
                 nc.scalar.activation(
-                    out=sq_tile(j)[:, 0:ws, :].rearrange("p (c i) t -> p c t i", i=4),
-                    in_=sq_source(j, 0, ws).rearrange("p t (c i) -> p c t i", i=4),
+                    out=sq_tile(j)[:, 0:ws, :].rearrange("p (c i) t -> p c t i", i=RUN),
+                    in_=sq_source(j, 0, ws).rearrange("p t (c i) -> p c t i", i=RUN),
                     func=ACT.Square,
                 )
 
@@ -200,9 +201,9 @@ def tile_einsumgdn_t_kernel(tc, x, beta, gamma, out):
             ws = sshare[j]
             we = pieces[j][3] - gshare[j]
             if ws < we:
-                vsrc = sq_source(j, ws, we).rearrange("p t (c i) -> p c t i", i=4)
+                vsrc = sq_source(j, ws, we).rearrange("p t (c i) -> p c t i", i=RUN)
                 nc.vector.tensor_tensor(
-                    out=sq_tile(j)[:, ws:we, :].rearrange("p (c i) t -> p c t i", i=4),
+                    out=sq_tile(j)[:, ws:we, :].rearrange("p (c i) t -> p c t i", i=RUN),
                     in0=vsrc, in1=vsrc, op=ALU.mult,
                 )
 

@@ -31,6 +31,7 @@ GRP_BUFS = 3
 RUN = 8
 QLEAD = 5
 NXB = 9
+FINE_FROM = 9
 
 
 def tile_einsumgdn_t_kernel(tc, x, beta, gamma, out):
@@ -347,8 +348,12 @@ def tile_einsumgdn_t_kernel(tc, x, beta, gamma, out):
             mm(k)
             rsq(k)
             if k >= 1:
-                finish(k - 1, 0, 2)
-                finish(k - 1, 2, 4)
+                if FINE_FROM <= k - 1:
+                    for b in range(4):
+                        finish(k - 1, b, b + 1)
+                else:
+                    finish(k - 1, 0, 2)
+                    finish(k - 1, 2, 4)
             if k < NXB:
                 xcopy(k)
             if k < 2:

@@ -105,11 +105,11 @@ def tile_einsumgdn_t_kernel(tc, x, beta, gamma, out):
             nc.sync.dma_start(out=bt[:], in_=beta_v)
         nc.sync.dma_start(out=xs[(1, 0)][:].rearrange("p j w -> p (j w)"), in_=x_v[1, 0])
         nc.sync.dma_start(out=graw[2][:], in_=gamma_v[1, 0])
+        nc.sync.dma_start(out=xs[(1, 1)][:].rearrange("p j w -> p (j w)"), in_=x_v[1, 1])
         nc.sync.dma_start(out=graw[3][:], in_=gamma_v[1, 1])
-        for n in range(1, NIMG):
+        for n in range(2, NIMG):
             for g in range(2):
-                if (n, g) != (1, 0):
-                    nc.sync.dma_start(out=xs[(n, g)][:].rearrange("p j w -> p (j w)"), in_=x_v[n, g])
+                nc.sync.dma_start(out=xs[(n, g)][:].rearrange("p j w -> p (j w)"), in_=x_v[n, g])
 
         warm = const.tile([P, 1], F32, name="warm")
         warm2 = const.tile([P, 1], F32, name="warm2")
@@ -338,6 +338,7 @@ def tile_einsumgdn_t_kernel(tc, x, beta, gamma, out):
         sq_vector(5)
         g_relu(2)
         sq_quant(4)
+        sq_vector(6)
 
         for k in range(NSLOT):
             if k < 3:
@@ -362,8 +363,8 @@ def tile_einsumgdn_t_kernel(tc, x, beta, gamma, out):
             if k < 3:
                 g_sub(k + 1, 0)
                 g_sub(k + 1, 1)
-            if k + QLEAD + 1 < npiece:
-                sq_vector(k + QLEAD + 1)
+            if k + QLEAD + 2 < npiece:
+                sq_vector(k + QLEAD + 2)
             if k < 3:
                 g_quant(k + 1)
             if k == 0:

@@ -29,6 +29,7 @@ NEND = 0
 WG = 208
 GRP_BUFS = 3
 RUN = 8
+PARTS = [(0, 0, 256), (0, 256, 256), (0, 512, 512), (1, 0, 1024)]
 QLEAD = 5
 NXB = 9
 FINE_FROM = 9
@@ -54,9 +55,9 @@ def tile_einsumgdn_t_kernel(tc, x, beta, gamma, out):
     for j in range(npiece):
         gshare.append(WG if j >= gfirst else 0)
         if j == 0:
-            sshare.append(256)
+            sshare.append(128)
         elif j == 1:
-            sshare.append(0)
+            sshare.append(128)
         elif j < 5:
             sshare.append(WS_HEAD)
         elif j < gfirst:
@@ -81,17 +82,22 @@ def tile_einsumgdn_t_kernel(tc, x, beta, gamma, out):
         for t in range(1, 4):
             graw[t] = gpool.tile([P, 2, C], BF16, name="graw", bufs=3)
         xpart = {}
-        for j in range(5):
-            xpart[j] = xpool.tile([P, 4, pieces[j][3]], BF16, name="xpart%d" % j)
+        for i in range(len(PARTS)):
+            xpart[i] = xpool.tile([P, 4, PARTS[i][2]], BF16, name="xpart%d" % i)
         xs = {}
         for n in range(1, NIMG):
             for g in range(2):
                 xs[(n, g)] = xpool.tile([P, 4, HW], BF16, name="xs%d%d" % (n, g))
         bt = const.tile([P, 2, 4], BF16, name="bt")
 
-        def load_part(j):
-            n, g, w0, wd = pieces[j]
-            nc.sync.dma_start(out=xpart[j][:], in_=x_c[0, g][:, :, w0 : w0 + wd])
+        def load_part(i):
+            g, w0, wd = PARTS[i]
+            nc.sync.dma_start(out=xpart[i][:], in_=x_c[0, g][:, :, w0 : w0 + wd])
+
+        def part_of(g, w):
+            for i, (pg, w0, wd) in enumerate(PARTS):
+                if pg == g and w0 <= w < w0 + wd:
+                    return xpart[i], w - w0
 
         nc.sync.dma_start(out=graw[(0, 0)][:], in_=gamma_v[0, 0][:, :, 0:512])
         load_part(0)
@@ -99,7 +105,6 @@ def tile_einsumgdn_t_kernel(tc, x, beta, gamma, out):
         load_part(1)
         load_part(2)
         load_part(3)
-        load_part(4)
         nc.sync.dma_start(out=graw[1][:], in_=gamma_v[0, 1])
         with nc.allow_non_contiguous_dma(reason="beta: four channels a partition, twice"):
             nc.sync.dma_start(out=bt[:], in_=beta_v)
@@ -186,7 +191,8 @@ def tile_einsumgdn_t_kernel(tc, x, beta, gamma, out):
         def sq_source(j, c0, c1):
             n, g, w0, wd = pieces[j]
             if n == 0:
-                return xpart[j][:, :, c0:c1]
+                part, p0 = part_of(g, w0 + c0)
+                return part[:, :, p0 : p0 + c1 - c0]
             return xs[(n, g)][:, :, w0 + c0 : w0 + c1]
 
         def sq_scalar(j):
@@ -255,13 +261,14 @@ def tile_einsumgdn_t_kernel(tc, x, beta, gamma, out):
                 bank = psum.tile([P, HW], BF16, name="aux")
                 xb[(k, e1)] = bank
                 if n == 0:
-                    for j in range(5):
-                        if pieces[j][1] == t // 2:
-                            w0, wd = pieces[j][2], pieces[j][3]
-                            nc.tensor.matmul(
-                                out=bank[:, w0 : w0 + wd], lhsT=identb[:], rhs=xpart[j][:, r0 + e1, :],
-                                start=True, stop=True,
-                            )
+                    for i, (pg, w0, wd) in enumerate(PARTS):
+                        if pg == t // 2:
+                            for c in range(0, wd, 512):
+                                cw = min(512, wd - c)
+                                nc.tensor.matmul(
+                                    out=bank[:, w0 + c : w0 + c + cw], lhsT=identb[:],
+                                    rhs=xpart[i][:, r0 + e1, c : c + cw], start=True, stop=True,
+                                )
                 else:
                     for h in range(2):
                         nc.tensor.matmul(
@@ -304,10 +311,12 @@ def tile_einsumgdn_t_kernel(tc, x, beta, gamma, out):
         g_relu((0, 0))
         g_transpose(0, 0)
         sq_scalar(0)
+        sq_vector(0)
         g_relu((0, 1))
         g_transpose(0, 1)
         g_square(0, 0)
         g_square(0, 1)
+        sq_scalar(1)
         sq_vector(1)
         sq_quant(0)
         sq_vector(2)
@@ -331,12 +340,12 @@ def tile_einsumgdn_t_kernel(tc, x, beta, gamma, out):
             out=bmax[:], in0=bt[:].rearrange("p g j -> p (g j)"),
             scalar1=BOUND_BETA, scalar2=None, op0=ALU.max,
         )
+        sq_vector(5)
         nc.vector.tensor_tensor(out=beff[:], in0=bmax[:], in1=bmax[:], op=ALU.mult)
+        g_relu(2)
         nc.vector.tensor_scalar(
             out=beff[:], in0=beff[:], scalar1=-PEDESTAL, scalar2=None, op0=ALU.add
         )
-        sq_vector(5)
-        g_relu(2)
         sq_quant(4)
         sq_vector(6)
 

@@ -22,7 +22,7 @@ BOUND_BETA = (1e-6 + PEDESTAL) ** 0.5
 
 NSLOT = 16
 WS_HEAD = 368
-WS_EARLY = 280
+WS_EARLY = 264
 WS_G = 224
 WS_END = 224
 NEND = 0
@@ -31,8 +31,8 @@ GRP_BUFS = 3
 RUN = 8
 PARTS = [(0, 0, 256), (0, 256, 256), (0, 512, 512), (1, 0, 1024)]
 QLEAD = 5
-NXB = 9
-FINE_FROM = 9
+NXB = 10
+FINE_FROM = 10
 
 
 def tile_einsumgdn_t_kernel(tc, x, beta, gamma, out):
@@ -49,7 +49,7 @@ def tile_einsumgdn_t_kernel(tc, x, beta, gamma, out):
             for h in range(2):
                 pieces.append((n, g, 512 * h, 512))
     npiece = len(pieces)
-    gfirst = QLEAD + GRP_BUFS
+    gfirst = QLEAD + 2
     sshare = []
     gshare = []
     for j in range(npiece):
@@ -207,6 +207,8 @@ def tile_einsumgdn_t_kernel(tc, x, beta, gamma, out):
         def sq_vector(j):
             ws = sshare[j]
             we = pieces[j][3] - gshare[j]
+            if gshare[j] > 0:
+                we += RUN
             if ws < we:
                 vsrc = sq_source(j, ws, we).rearrange("p t (c i) -> p c t i", i=RUN)
                 nc.vector.tensor_tensor(
@@ -372,15 +374,14 @@ def tile_einsumgdn_t_kernel(tc, x, beta, gamma, out):
             if k < 3:
                 g_sub(k + 1, 0)
                 g_sub(k + 1, 1)
-            if k + QLEAD + 2 < npiece:
-                sq_vector(k + QLEAD + 2)
-            if k < 3:
-                g_quant(k + 1)
             if k == 0:
                 g_relu(3)
             if k + QLEAD < npiece:
                 sq_quant(k + QLEAD)
-                if k + QLEAD + GRP_BUFS < npiece:
-                    sq_gpsimd(k + QLEAD + GRP_BUFS)
+                if k < 3:
+                    g_quant(k + 1)
+                if k + QLEAD + 2 < npiece:
+                    sq_vector(k + QLEAD + 2)
+                    sq_gpsimd(k + QLEAD + 2)
         for b in range(4):
             finish(NSLOT - 1, b, b + 1)

@@ -32,6 +32,7 @@ RUN = 8
 PARTS = [(0, 0, 256), (0, 256, 256), (0, 512, 512), (1, 0, 1024)]
 QLEAD = 5
 NXB = 10
+FINE_STORE = 14
 FINE_FROM = 10
 
 
@@ -308,7 +309,11 @@ def tile_einsumgdn_t_kernel(tc, x, beta, gamma, out):
                 nc.vector.tensor_tensor(
                     out=otile[k][:, cols], in0=otile[k][:, cols], in1=xrow[:, cols], op=ALU.mult
                 )
-            nc.sync.dma_start(out=out_v[n, t // 2, t % 2][:, cols], in_=otile[k][:, cols])
+            if k < FINE_FROM or k >= FINE_STORE:
+                nc.sync.dma_start(out=out_v[n, t // 2, t % 2][:, cols], in_=otile[k][:, cols])
+            elif b1 % 2 == 0:
+                cols = slice(512 * b1 - 1024, 512 * b1)
+                nc.sync.dma_start(out=out_v[n, t // 2, t % 2][:, cols], in_=otile[k][:, cols])
 
         g_relu((0, 0))
         g_transpose(0, 0)

@@ -243,7 +243,7 @@ def tile_einsumgdn_t_kernel(tc, x, beta, gamma, out):
             n, t = k // 4, k % 4
             for e1 in range(2):
                 for h in range(2):
-                    bank = psum.tile([P, 512], F32, name="acc")
+                    bank = psum.tile([P, 512], F32, name="aux" if k > NXB and k % 2 == 0 else "acc")
                     acc[(k, e1, h)] = bank
                     for g in range(2):
                         m0 = 256 * g + 128 * e1

@@ -22,9 +22,9 @@ BOUND_BETA = (1e-6 + PEDESTAL) ** 0.5
 
 NSLOT = 16
 WS_HEAD = 368
-WS_EARLY = 264
-WS_G = 224
-WS_END = 224
+WS_EARLY = 280
+WS_G = 240
+WS_END = 240
 NEND = 0
 WG = 208
 GRP_BUFS = 3

from contextlib import ExitStack

import concourse.mybir as mybir
from concourse.masks import make_identity

F32 = mybir.dt.float32
BF16 = mybir.dt.bfloat16
U32 = mybir.dt.uint32
U8 = mybir.dt.uint8
FP8X4 = mybir.dt.float8_e4m3fn_x4
ALU = mybir.AluOpType
ACT = mybir.ActivationFunctionType

P = 128
NIMG = 4
C = 1024
HW = 1024
FLOPS = 2 * NIMG * C * C * HW

PEDESTAL = 2.0 ** -36
BOUND_BETA = (1e-6 + PEDESTAL) ** 0.5

NSLOT = 16
WS_HEAD = 368
WS_EARLY = 280
WS_G = 240
WS_END = 240
NEND = 0
WG = 208
GRP_BUFS = 3
RUN = 8
PARTS = [(0, 0, 256), (0, 256, 256), (0, 512, 512), (1, 0, 1024)]
QLEAD = 5
NXB = 10
FINE_STORE = 14
FINE_FROM = 10


def tile_einsumgdn_t_kernel(tc, x, beta, gamma, out):
    nc = tc.nc
    x_v = x.rearrange("n (g p j) h w -> n g p (j h w)", g=2, p=P, j=4)
    x_c = x.rearrange("n (g p j) h w -> n g p j (h w)", g=2, p=P, j=4)
    out_v = out.rearrange("n (g p s e) h w -> n g s p (e h w)", g=2, p=P, s=2, e=2)
    gamma_v = gamma.rearrange("(g p s e) c -> g s p e c", g=2, p=P, s=2, e=2)
    beta_v = beta.rearrange("(g p j) -> p g j", g=2, p=P, j=4)

    pieces = [(0, 0, 0, 256), (0, 0, 256, 256), (0, 0, 512, 512), (0, 1, 0, 512), (0, 1, 512, 512)]
    for n in range(1, NIMG):
        for g in range(2):
            for h in range(2):
                pieces.append((n, g, 512 * h, 512))
    npiece = len(pieces)
    gfirst = QLEAD + 2
    sshare = []
    gshare = []
    for j in range(npiece):
        gshare.append(WG if j >= gfirst else 0)
        if j == 0:
            sshare.append(128)
        elif j == 1:
            sshare.append(128)
        elif j < 5:
            sshare.append(WS_HEAD)
        elif j < gfirst:
            sshare.append(WS_EARLY)
        elif j < npiece - NEND:
            sshare.append(WS_G)
        else:
            sshare.append(WS_END)

    with ExitStack() as ctx:
        const = ctx.enter_context(tc.tile_pool(name="const", bufs=1))
        xpool = ctx.enter_context(tc.tile_pool(name="xpool", bufs=1))
        gpool = ctx.enter_context(tc.tile_pool(name="gpool", bufs=2))
        work = ctx.enter_context(tc.tile_pool(name="work", bufs=3))
        opool = ctx.enter_context(tc.tile_pool(name="opool", bufs=5))
        psum = ctx.enter_context(tc.psum_pool(name="psum", bufs=4))
        ctx.enter_context(tc.manual_schedule())

        graw = {}
        for g in range(2):
            graw[(0, g)] = gpool.tile([P, 2, 512], BF16, name="graw0%d" % g, bufs=1)
        for t in range(1, 4):
            graw[t] = gpool.tile([P, 2, C], BF16, name="graw", bufs=3)
        xpart = {}
        for i in range(len(PARTS)):
            xpart[i] = xpool.tile([P, 4, PARTS[i][2]], BF16, name="xpart%d" % i)
        xs = {}
        for n in range(1, NIMG):
            for g in range(2):
                xs[(n, g)] = xpool.tile([P, 4, HW], BF16, name="xs%d%d" % (n, g))
        bt = const.tile([P, 2, 4], BF16, name="bt")

        def load_part(i):
            g, w0, wd = PARTS[i]
            nc.sync.dma_start(out=xpart[i][:], in_=x_c[0, g][:, :, w0 : w0 + wd])

        def part_of(g, w):
            for i, (pg, w0, wd) in enumerate(PARTS):
                if pg == g and w0 <= w < w0 + wd:
                    return xpart[i], w - w0

        nc.sync.dma_start(out=graw[(0, 0)][:], in_=gamma_v[0, 0][:, :, 0:512])
        load_part(0)
        nc.sync.dma_start(out=graw[(0, 1)][:], in_=gamma_v[0, 0][:, :, 512:1024])
        load_part(1)
        load_part(2)
        load_part(3)
        nc.sync.dma_start(out=graw[1][:], in_=gamma_v[0, 1])
        with nc.allow_non_contiguous_dma(reason="beta: four channels a partition, twice"):
            nc.sync.dma_start(out=bt[:], in_=beta_v)
        nc.sync.dma_start(out=xs[(1, 0)][:].rearrange("p j w -> p (j w)"), in_=x_v[1, 0])
        nc.sync.dma_start(out=graw[2][:], in_=gamma_v[1, 0])
        nc.sync.dma_start(out=xs[(1, 1)][:].rearrange("p j w -> p (j w)"), in_=x_v[1, 1])
        nc.sync.dma_start(out=graw[3][:], in_=gamma_v[1, 1])
        for n in range(2, NIMG):
            for g in range(2):
                nc.sync.dma_start(out=xs[(n, g)][:].rearrange("p j w -> p (j w)"), in_=x_v[n, g])

        warm = const.tile([P, 1], F32, name="warm")
        warm2 = const.tile([P, 1], F32, name="warm2")
        nc.vector.memset(warm[:], 1.0)
        nc.scalar.activation(out=warm2[:], in_=warm[:], func=ACT.Abs_reciprocal_sqrt)

        ident = const.tile([P, P], F32, name="ident")
        make_identity(nc, ident[:])
        identb = const.tile([P, P], BF16, name="identb")
        make_identity(nc, identb[:])

        gcodes = const.tile([P, 4, 512], U32, name="gcodes", align_bytes=64)
        gsc = const.tile([P, 4, 512], U8, name="gsc", align_bytes=64)
        grelu = {}
        gbank = {}
        gsq = {}
        gg = {}

        def g_relu(key):
            if key in (1, 2, 3):
                grelu[key] = gpool.tile([P, 2, C], BF16, name="grelu", bufs=3)
            else:
                grelu[key] = gpool.tile([P, 2, 512], BF16, name="grelu0%d" % key[1], bufs=1)
            nc.vector.tensor_scalar(
                out=grelu[key][:], in0=graw[key][:], scalar1=0.0, scalar2=None, op0=ALU.max
            )

        def g_transpose(t, g):
            src = grelu[(0, g)] if t == 0 else grelu[t]
            gw = src[:].rearrange("p e c -> p (e c)").bitcast(F32)
            bank = psum.tile([P, 512], F32, name="aux")
            for u in range(2):
                for e1 in range(2):
                    src0 = (256 * e1) if t == 0 else (512 * e1 + 256 * g)
                    dst0 = 256 * u + 128 * e1
                    nc.tensor.transpose(
                        bank[:, dst0 : dst0 + 128], gw[:, src0 + u : src0 + 256 : 2], ident[:]
                    )
            gbank[(t, g)] = bank

        def g_square(t, g):
            sq = work.tile([P, 1024], F32, name="sq", bufs=4)
            nc.scalar.activation(
                out=sq[:].rearrange("p (j u e) -> p j u e", u=2, e=2),
                in_=gbank[(t, g)][:].bitcast(BF16).rearrange("p (u j e) -> p j u e", u=2, e=2),
                func=ACT.Square,
            )
            gsq[(t, g)] = sq

        def g_sub(t, g):
            if g == 0:
                gg[t] = gpool.tile([P, 2, 1024], BF16, name="gg", bufs=3, align_bytes=64)
            nc.vector.tensor_scalar(
                out=gg[t][:, g, :], in0=gsq[(t, g)][:], scalar1=-PEDESTAL, scalar2=0.0,
                op0=ALU.add, op1=ALU.max,
            )

        def g_quant(t):
            nc.vector.quantize_mx(
                out=gcodes[:, t, :].bitcast(FP8X4),
                scales=gsc[:, t, :],
                in_=gg[t][:].rearrange("p g k -> p (g k)"),
            )

        xcodes = {}
        xsc = {}
        grp = {}

        def sq_tile(j):
            if j not in grp:
                grp[j] = work.tile([P, 512, 4], BF16, name="grp", bufs=GRP_BUFS, align_bytes=64)
            return grp[j]

        def sq_source(j, c0, c1):
            n, g, w0, wd = pieces[j]
            if n == 0:
                part, p0 = part_of(g, w0 + c0)
                return part[:, :, p0 : p0 + c1 - c0]
            return xs[(n, g)][:, :, w0 + c0 : w0 + c1]

        def sq_scalar(j):
            ws = sshare[j]
            if ws > 0:
                nc.scalar.activation(
                    out=sq_tile(j)[:, 0:ws, :].rearrange("p (c i) t -> p c t i", i=RUN),
                    in_=sq_source(j, 0, ws).rearrange("p t (c i) -> p c t i", i=RUN),
                    func=ACT.Square,
                )

        def sq_vector(j):
            ws = sshare[j]
            we = pieces[j][3] - gshare[j]
            if gshare[j] > 0:
                we += RUN
            if ws < we:
                vsrc = sq_source(j, ws, we).rearrange("p t (c i) -> p c t i", i=RUN)
                nc.vector.tensor_tensor(
                    out=sq_tile(j)[:, ws:we, :].rearrange("p (c i) t -> p c t i", i=RUN),
                    in0=vsrc, in1=vsrc, op=ALU.mult,
                )

        def sq_gpsimd(j):
            wd = pieces[j][3]
            gsrc = sq_source(j, wd - gshare[j], wd).rearrange("p t w -> p w t")
            nc.gpsimd.tensor_tensor(
                out=sq_tile(j)[:, wd - gshare[j] : wd, :], in0=gsrc, in1=gsrc, op=ALU.mult
            )

        def sq_quant(j):
            n, g, w0, wd = pieces[j]
            if n not in xcodes:
                xcodes[n] = work.tile([P, 2, HW], U32, name="xcodes", align_bytes=64)
                xsc[n] = work.tile([P, 2, HW], U8, name="xsc", align_bytes=64)
            nc.vector.quantize_mx(
                out=xcodes[n][:, g, w0 : w0 + wd].bitcast(FP8X4),
                scales=xsc[n][:, g, w0 : w0 + wd],
                in_=grp[j][:, 0:wd, :].rearrange("p w t -> p (w t)"),
            )

        acc = {}
        otile = {}
        xb = {}

        def mm(k):
            n, t = k // 4, k % 4
            for e1 in range(2):
                for h in range(2):
                    bank = psum.tile([P, 512], F32, name="aux" if k > NXB and k % 2 == 0 else "acc")
                    acc[(k, e1, h)] = bank
                    for g in range(2):
                        m0 = 256 * g + 128 * e1
                        nc.tensor.matmul_mx(
                            out=bank[:],
                            lhsT=gcodes[:, t, m0 : m0 + 128].bitcast(FP8X4),
                            lhsT_scale=gsc[:, t, m0 : m0 + 128],
                            rhs=xcodes[n][:, g, 512 * h : 512 * h + 512].bitcast(FP8X4),
                            rhs_scale=xsc[n][:, g, 512 * h : 512 * h + 512],
                            start=(g == 0),
                            stop=(g == 1),
                        )

        def xcopy(k):
            n, t = k // 4, k % 4
            r0 = 2 * (t % 2)
            for e1 in range(2):
                bank = psum.tile([P, HW], BF16, name="aux")
                xb[(k, e1)] = bank
                if n == 0:
                    for i, (pg, w0, wd) in enumerate(PARTS):
                        if pg == t // 2:
                            for c in range(0, wd, 512):
                                cw = min(512, wd - c)
                                nc.tensor.matmul(
                                    out=bank[:, w0 + c : w0 + c + cw], lhsT=identb[:],
                                    rhs=xpart[i][:, r0 + e1, c : c + cw], start=True, stop=True,
                                )
                else:
                    for h in range(2):
                        nc.tensor.matmul(
                            out=bank[:, 512 * h : 512 * h + 512], lhsT=identb[:],
                            rhs=xs[(n, t // 2)][:, r0 + e1, 512 * h : 512 * h + 512],
                            start=True, stop=True,
                        )

        def rsq(k):
            t = k % 4
            otile[k] = opool.tile([P, 2 * HW], F32, name="o")
            for e1 in range(2):
                for h in range(2):
                    c0 = HW * e1 + 512 * h
                    nc.scalar.activation(
                        out=otile[k][:, c0 : c0 + 512],
                        in_=acc[(k, e1, h)][:],
                        func=ACT.Abs_reciprocal_sqrt,
                        bias=beff[:, 2 * t + e1 : 2 * t + e1 + 1],
                        scale=1.0,
                    )

        def finish(k, b0, b1):
            n, t = k // 4, k % 4
            r0 = 2 * (t % 2)
            cols = slice(512 * b0, 512 * b1)
            if k < NXB:
                for e1 in range(b0 // 2, b1 // 2):
                    row = slice(HW * e1, HW * e1 + HW)
                    nc.vector.tensor_tensor(
                        out=otile[k][:, row], in0=otile[k][:, row], in1=xb[(k, e1)][:], op=ALU.mult
                    )
            else:
                xrow = xs[(n, t // 2)][:, r0 : r0 + 2, :].rearrange("p e w -> p (e w)")
                nc.vector.tensor_tensor(
                    out=otile[k][:, cols], in0=otile[k][:, cols], in1=xrow[:, cols], op=ALU.mult
                )
            if k < FINE_FROM or k >= FINE_STORE:
                nc.sync.dma_start(out=out_v[n, t // 2, t % 2][:, cols], in_=otile[k][:, cols])
            elif b1 % 2 == 0:
                cols = slice(512 * b1 - 1024, 512 * b1)
                nc.sync.dma_start(out=out_v[n, t // 2, t % 2][:, cols], in_=otile[k][:, cols])

        g_relu((0, 0))
        g_transpose(0, 0)
        sq_scalar(0)
        sq_vector(0)
        g_relu((0, 1))
        g_transpose(0, 1)
        g_square(0, 0)
        g_square(0, 1)
        sq_scalar(1)
        sq_vector(1)
        sq_quant(0)
        sq_vector(2)
        sq_scalar(2)
        g_sub(0, 0)
        sq_quant(1)
        g_sub(0, 1)
        sq_vector(3)
        sq_scalar(3)
        sq_quant(2)
        g_quant(0)
        g_relu(1)
        g_transpose(1, 0)
        g_transpose(1, 1)
        sq_vector(4)
        sq_scalar(4)
        sq_quant(3)
        bmax = const.tile([P, 8], F32, name="bmax")
        beff = const.tile([P, 8], F32, name="beff")
        nc.vector.tensor_scalar(
            out=bmax[:], in0=bt[:].rearrange("p g j -> p (g j)"),
            scalar1=BOUND_BETA, scalar2=None, op0=ALU.max,
        )
        sq_vector(5)
        nc.vector.tensor_tensor(out=beff[:], in0=bmax[:], in1=bmax[:], op=ALU.mult)
        g_relu(2)
        nc.vector.tensor_scalar(
            out=beff[:], in0=beff[:], scalar1=-PEDESTAL, scalar2=None, op0=ALU.add
        )
        sq_quant(4)
        sq_vector(6)

        for k in range(NSLOT):
            if k < 3:
                g_square(k + 1, 0)
                g_square(k + 1, 1)
            if k + QLEAD < npiece:
                sq_scalar(k + QLEAD)
            mm(k)
            rsq(k)
            if k >= 1:
                if FINE_FROM <= k - 1:
                    for b in range(4):
                        finish(k - 1, b, b + 1)
                else:
                    finish(k - 1, 0, 2)
                    finish(k - 1, 2, 4)
            if k < NXB:
                xcopy(k)
            if k < 2:
                g_transpose(k + 2, 0)
                g_transpose(k + 2, 1)
            if k < 3:
                g_sub(k + 1, 0)
                g_sub(k + 1, 1)
            if k == 0:
                g_relu(3)
            if k + QLEAD < npiece:
                sq_quant(k + QLEAD)
                if k < 3:
                    g_quant(k + 1)
                if k + QLEAD + 2 < npiece:
                    sq_vector(k + QLEAD + 2)
                    sq_gpsimd(k + QLEAD + 2)
        for b in range(4):
            finish(NSLOT - 1, b, b + 1)
